import numpy as np
import ml_dtypes

BF16 = ml_dtypes.bfloat16


def bf(x):
    return np.asarray(x, np.float32).astype(BF16)


def f32(x):
    return np.asarray(x, np.float32)


def f64(x):
    return np.asarray(x).astype(np.float64)


def striped(idx):
    return np.tile(idx.reshape(-1, 16).T, (8, 1))


C, S, N, F = 512, 2048, 1024, 2048
EPS = 1e-5


def setup_inputs():
    return {"emb": f32(np.random.standard_normal((C, S))), "gain": f32(1.0 + 0.1 * np.random.standard_normal((C, 1))), "shift": f32(0.1 * np.random.standard_normal((C, 1))), "w_x": bf(np.random.standard_normal((C, F)) / np.sqrt(C)), "w_gate": bf(np.random.standard_normal((C, F)) / np.sqrt(C)), "w_ff": bf(np.random.standard_normal((F, C)) / np.sqrt(F)), "offs": striped(np.random.permutation(S)[:N])}


def reference(emb, gain, shift, w_x, w_gate, w_ff, offs):
    idx = offs[:16].T.reshape(-1)
    x = f64(emb)[:, idx]
    mu = x.mean(axis=0, keepdims=True)
    var = ((x - mu) ** 2).mean(axis=0, keepdims=True)
    h = (x - mu) / np.sqrt(var + EPS) * f64(gain) + f64(shift)
    u = f64(w_x).T @ h
    z = f64(w_gate).T @ h
    a = z / (1.0 + np.exp(-z)) * u
    return x + f64(w_ff).T @ a

@@ -1,0 +1,155 @@
+from contextlib import ExitStack
+
+import concourse.mybir as mybir
+
+C, S, N, F = 512, 2048, 1024, 2048
+EPS = 1e-5
+P = 128
+KB = C // P
+FB = F // P
+W = 512
+CHUNKS = N // W
+GROUP = 4
+FLOPS = 2 * C * F * N * 3
+
+F32 = mybir.dt.float32
+BF16 = mybir.dt.bfloat16
+U16 = mybir.dt.uint16
+ACT = mybir.ActivationFunctionType
+ALU = mybir.AluOpType
+
+
+def tile_textencoder_b_kernel(tc, emb, gain, shift, w_x, w_gate, w_ff, offs, out):
+    nc = tc.nc
+    with ExitStack() as ctx:
+        held = ctx.enter_context(tc.tile_pool(name="held", bufs=1))
+        norm = ctx.enter_context(tc.tile_pool(name="norm", bufs=2))
+        block = ctx.enter_context(tc.tile_pool(name="block", bufs=4))
+        mlp = ctx.enter_context(tc.tile_pool(name="mlp", bufs=2))
+        stage = ctx.enter_context(tc.tile_pool(name="stage", bufs=3))
+        stat_psum = ctx.enter_context(tc.psum_pool(name="stat_psum", bufs=1))
+        up_psum = ctx.enter_context(tc.psum_pool(name="up_psum", bufs=2))
+        down_psum = ctx.enter_context(tc.psum_pool(name="down_psum", bufs=2))
+
+        offsets = held.tile([P, N // 16], U16, name="offsets")
+        nc.sync.dma_start(offsets[:], offs)
+        table = []
+        for kb in range(KB):
+            table_kb = held.tile([P, S], F32, name=f"table{kb}")
+            nc.sync.dma_start(table_kb[:], emb[kb * P : (kb + 1) * P, :])
+            table.append(table_kb)
+
+        gain_sb = held.tile([P, KB], F32, name="gain_sb")
+        shift_sb = held.tile([P, KB], F32, name="shift_sb")
+        with nc.allow_non_contiguous_dma(reason="512 single floats, one to a partition and block"):
+            nc.scalar.dma_start(gain_sb[:], gain.rearrange("(k p) o -> p (k o)", p=P))
+            nc.scalar.dma_start(shift_sb[:], shift.rearrange("(k p) o -> p (k o)", p=P))
+
+        w_gate_view = w_gate.rearrange("(k p) f -> p k f", p=P)
+        w_x_view = w_x.rearrange("(k p) f -> p k f", p=P)
+        w_ff_view = w_ff.rearrange("(b p) c -> p b c", p=P)
+        wg, wx, wf = [], [], []
+        for g in range(FB // GROUP):
+            f_cols = slice(g * GROUP * P, (g + 1) * GROUP * P)
+            wg_g = held.tile([P, KB, GROUP * P], BF16, name=f"wg{g}")
+            nc.sync.dma_start(wg_g[:], w_gate_view[:, :, f_cols])
+            wg.append(wg_g)
+            wx_g = held.tile([P, KB, GROUP * P], BF16, name=f"wx{g}")
+            nc.sync.dma_start(wx_g[:], w_x_view[:, :, f_cols])
+            wx.append(wx_g)
+        for g in range(FB // GROUP):
+            wf_g = held.tile([P, GROUP, C], BF16, name=f"wf{g}")
+            nc.sync.dma_start(wf_g[:], w_ff_view[:, g * GROUP : (g + 1) * GROUP, :])
+            wf.append(wf_g)
+
+        averager = held.tile([P, P], F32, name="averager")
+        nc.vector.memset(averager[:], 1.0 / C)
+        eps_sb = held.tile([P, 1], F32, name="eps_sb")
+        nc.vector.memset(eps_sb[:], EPS)
+
+        x = [held.tile([P, N], F32, name=f"x{kb}") for kb in range(KB)]
+
+        def chunk_cols(t):
+            return slice(t * W, (t + 1) * W)
+
+        def look_up(t):
+            piece = offsets[:, t * (W // 16) : (t + 1) * (W // 16)]
+            for kb in range(KB):
+                nc.scalar.activation(x[kb][:, chunk_cols(t)], table[kb][:].indirect(piece), ACT.Copy)
+
+        def centre_and_square(t):
+            cols = chunk_cols(t)
+            x_sum = norm.tile([P, W], F32, name="x_sum")
+            nc.vector.tensor_tensor(x_sum[:], x[0][:, cols], x[1][:, cols], ALU.add)
+            for kb in range(2, KB):
+                nc.vector.tensor_tensor(x_sum[:], x_sum[:], x[kb][:, cols], ALU.add)
+            mean_ps = stat_psum.tile([P, W], F32, name="mean_ps")
+            nc.tensor.matmul(mean_ps[:], averager[:], x_sum[:], start=True, stop=True)
+
+            centred = norm.tile([P, KB, W], F32, name="centred")
+            squares = []
+            for kb in range(KB):
+                nc.vector.tensor_tensor(centred[:, kb, :], x[kb][:, cols], mean_ps[:], ALU.subtract)
+                square = block.tile([P, W], F32, name="square")
+                nc.scalar.activation(square[:], centred[:, kb, :], ACT.Square)
+                squares.append(square)
+            square_sum = norm.tile([P, W], F32, name="square_sum")
+            nc.vector.tensor_tensor(square_sum[:], squares[0][:], squares[1][:], ALU.add)
+            for kb in range(2, KB):
+                nc.vector.tensor_tensor(square_sum[:], square_sum[:], squares[kb][:], ALU.add)
+            return centred, square_sum
+
+        def normalise(centred, square_sum):
+            var_ps = stat_psum.tile([P, W], F32, name="var_ps")
+            nc.tensor.matmul(var_ps[:], averager[:], square_sum[:], start=True, stop=True)
+            rstd = norm.tile([P, W], F32, name="rstd")
+            nc.scalar.activation(rstd[:], var_ps[:], ACT.Abs_reciprocal_sqrt, bias=eps_sb[:, 0:1])
+            h = norm.tile([P, KB, W], BF16, name="h")
+            for kb in range(KB):
+                unit = block.tile([P, W], F32, name="unit")
+                nc.vector.tensor_tensor(unit[:], centred[:, kb, :], rstd[:], ALU.mult)
+                nc.scalar.activation(
+                    h[:, kb, :], unit[:], ACT.Identity, bias=shift_sb[:, kb : kb + 1], scale=gain_sb[:, kb : kb + 1]
+                )
+            return h
+
+        def up(h):
+            gated = mlp.tile([P, FB, W], BF16, name="gated")
+            for fb in range(FB):
+                g, i = divmod(fb, GROUP)
+                f_cols = slice(i * P, (i + 1) * P)
+                z_ps = up_psum.tile([P, W], F32, name="z_ps")
+                for kb in range(KB):
+                    nc.tensor.matmul(z_ps[:], wg[g][:, kb, f_cols], h[:, kb, :], start=(kb == 0), stop=(kb == KB - 1))
+                u_ps = up_psum.tile([P, W], F32, name="u_ps")
+                for kb in range(KB):
+                    nc.tensor.matmul(u_ps[:], wx[g][:, kb, f_cols], h[:, kb, :], start=(kb == 0), stop=(kb == KB - 1))
+                silu = stage.tile([P, W], F32, name="silu")
+                nc.scalar.activation(silu[:], z_ps[:], ACT.Silu)
+                nc.vector.tensor_tensor(gated[:, fb, :], silu[:], u_ps[:], ALU.mult)
+            return gated
+
+        def down(t, gated):
+            cols = chunk_cols(t)
+            for cb in range(KB):
+                o_ps = down_psum.tile([P, W], F32, name="o_ps")
+                for fb in range(FB):
+                    g, i = divmod(fb, GROUP)
+                    nc.tensor.matmul(
+                        o_ps[:], wf[g][:, i, cb * P : (cb + 1) * P], gated[:, fb, :], start=(fb == 0), stop=(fb == FB - 1)
+                    )
+                result = stage.tile([P, W], F32, name="result")
+                nc.vector.tensor_tensor(result[:], o_ps[:], x[cb][:, cols], ALU.add)
+                nc.sync.dma_start(out[cb * P : (cb + 1) * P, cols], result[:])
+
+        look_up(0)
+        h = normalise(*centre_and_square(0))
+        for t in range(1, CHUNKS):
+            look_up(t)
+        for t in range(CHUNKS):
+            if t + 1 < CHUNKS:
+                half_done = centre_and_square(t + 1)
+            gated = up(h)
+            if t + 1 < CHUNKS:
+                h = normalise(*half_done)
+            down(t, gated)

@@ -7,7 +7,7 @@ EPS = 1e-5
 P = 128
 KB = C // P
 FB = F // P
-W = 512
+W = 256
 CHUNKS = N // W
 GROUP = 4
 FLOPS = 2 * C * F * N * 3
@@ -23,6 +23,7 @@ def tile_textencoder_b_kernel(tc, emb, gain, shift, w_x, w_gate, w_ff, offs, out
     nc = tc.nc
     with ExitStack() as ctx:
         held = ctx.enter_context(tc.tile_pool(name="held", bufs=1))
+        looked_up = ctx.enter_context(tc.tile_pool(name="looked_up", bufs=2))
         norm = ctx.enter_context(tc.tile_pool(name="norm", bufs=2))
         block = ctx.enter_context(tc.tile_pool(name="block", bufs=4))
         mlp = ctx.enter_context(tc.tile_pool(name="mlp", bufs=2))
@@ -67,41 +68,40 @@ def tile_textencoder_b_kernel(tc, emb, gain, shift, w_x, w_gate, w_ff, offs, out
         eps_sb = held.tile([P, 1], F32, name="eps_sb")
         nc.vector.memset(eps_sb[:], EPS)
 
-        x = [held.tile([P, N], F32, name=f"x{kb}") for kb in range(KB)]
-
-        def chunk_cols(t):
-            return slice(t * W, (t + 1) * W)
-
         def look_up(t):
+            x = looked_up.tile([P, KB, W], F32, name="x")
             piece = offsets[:, t * (W // 16) : (t + 1) * (W // 16)]
             for kb in range(KB):
-                nc.scalar.activation(x[kb][:, chunk_cols(t)], table[kb][:].indirect(piece), ACT.Copy)
+                nc.scalar.activation(x[:, kb, :], table[kb][:].indirect(piece), ACT.Copy)
+            return x
 
-        def centre_and_square(t):
-            cols = chunk_cols(t)
-            x_sum = norm.tile([P, W], F32, name="x_sum")
-            nc.vector.tensor_tensor(x_sum[:], x[0][:, cols], x[1][:, cols], ALU.add)
-            for kb in range(2, KB):
-                nc.vector.tensor_tensor(x_sum[:], x_sum[:], x[kb][:, cols], ALU.add)
-            mean_ps = stat_psum.tile([P, W], F32, name="mean_ps")
-            nc.tensor.matmul(mean_ps[:], averager[:], x_sum[:], start=True, stop=True)
+        def add_up(parts):
+            total = norm.tile([P, W], F32, name="total")
+            nc.vector.tensor_tensor(total[:], parts[0], parts[1], ALU.add)
+            for part in parts[2:]:
+                nc.vector.tensor_tensor(total[:], total[:], part, ALU.add)
+            return [total[:]]
 
+        def average(parts, name):
+            mean_ps = stat_psum.tile([P, W], F32, name=name)
+            for i, part in enumerate(parts):
+                nc.tensor.matmul(mean_ps[:], averager[:], part, start=(i == 0), stop=(i == len(parts) - 1))
+            return mean_ps
+
+        def centre_and_square(x, tensor_engine_adds):
+            blocks = [x[:, kb, :] for kb in range(KB)]
+            mean_ps = average(blocks if tensor_engine_adds else add_up(blocks), "mean_ps")
             centred = norm.tile([P, KB, W], F32, name="centred")
             squares = []
             for kb in range(KB):
-                nc.vector.tensor_tensor(centred[:, kb, :], x[kb][:, cols], mean_ps[:], ALU.subtract)
+                nc.vector.tensor_tensor(centred[:, kb, :], blocks[kb], mean_ps[:], ALU.subtract)
                 square = block.tile([P, W], F32, name="square")
                 nc.scalar.activation(square[:], centred[:, kb, :], ACT.Square)
-                squares.append(square)
-            square_sum = norm.tile([P, W], F32, name="square_sum")
-            nc.vector.tensor_tensor(square_sum[:], squares[0][:], squares[1][:], ALU.add)
-            for kb in range(2, KB):
-                nc.vector.tensor_tensor(square_sum[:], square_sum[:], squares[kb][:], ALU.add)
-            return centred, square_sum
+                squares.append(square[:])
+            return centred, (squares if tensor_engine_adds else add_up(squares))
 
-        def normalise(centred, square_sum):
-            var_ps = stat_psum.tile([P, W], F32, name="var_ps")
-            nc.tensor.matmul(var_ps[:], averager[:], square_sum[:], start=True, stop=True)
+        def normalise(centred, squares):
+            var_ps = average(squares, "var_ps")
             rstd = norm.tile([P, W], F32, name="rstd")
             nc.scalar.activation(rstd[:], var_ps[:], ACT.Abs_reciprocal_sqrt, bias=eps_sb[:, 0:1])
             h = norm.tile([P, KB, W], BF16, name="h")
@@ -113,9 +113,8 @@ def tile_textencoder_b_kernel(tc, emb, gain, shift, w_x, w_gate, w_ff, offs, out
                 )
             return h
 
-        def up(h):
-            gated = mlp.tile([P, FB, W], BF16, name="gated")
-            for fb in range(FB):
+        def up(h, gated, hidden_blocks):
+            for fb in hidden_blocks:
                 g, i = divmod(fb, GROUP)
                 f_cols = slice(i * P, (i + 1) * P)
                 z_ps = up_psum.tile([P, W], F32, name="z_ps")
@@ -127,10 +126,8 @@ def tile_textencoder_b_kernel(tc, emb, gain, shift, w_x, w_gate, w_ff, offs, out
                 silu = stage.tile([P, W], F32, name="silu")
                 nc.scalar.activation(silu[:], z_ps[:], ACT.Silu)
                 nc.vector.tensor_tensor(gated[:, fb, :], silu[:], u_ps[:], ALU.mult)
-            return gated
 
-        def down(t, gated):
-            cols = chunk_cols(t)
+        def down(t, x, gated):
             for cb in range(KB):
                 o_ps = down_psum.tile([P, W], F32, name="o_ps")
                 for fb in range(FB):
@@ -139,17 +136,21 @@ def tile_textencoder_b_kernel(tc, emb, gain, shift, w_x, w_gate, w_ff, offs, out
                         o_ps[:], wf[g][:, i, cb * P : (cb + 1) * P], gated[:, fb, :], start=(fb == 0), stop=(fb == FB - 1)
                     )
                 result = stage.tile([P, W], F32, name="result")
-                nc.vector.tensor_tensor(result[:], o_ps[:], x[cb][:, cols], ALU.add)
-                nc.sync.dma_start(out[cb * P : (cb + 1) * P, cols], result[:])
+                nc.vector.tensor_tensor(result[:], o_ps[:], x[:, cb, :], ALU.add)
+                nc.sync.dma_start(out[cb * P : (cb + 1) * P, t * W : (t + 1) * W], result[:])
 
-        look_up(0)
-        h = normalise(*centre_and_square(0))
-        for t in range(1, CHUNKS):
-            look_up(t)
+        x = look_up(0)
+        h = normalise(*centre_and_square(x, tensor_engine_adds=True))
         for t in range(CHUNKS):
-            if t + 1 < CHUNKS:
-                half_done = centre_and_square(t + 1)
-            gated = up(h)
-            if t + 1 < CHUNKS:
+            last = t == CHUNKS - 1
+            gated = mlp.tile([P, FB, W], BF16, name="gated")
+            up(h, gated, range(0, FB // 2))
+            if not last:
+                x_next = look_up(t + 1)
+                half_done = centre_and_square(x_next, tensor_engine_adds=False)
+            up(h, gated, range(FB // 2, FB))
+            if not last:
                 h = normalise(*half_done)
-            down(t, gated)
+            down(t, x, gated)
+            if not last:
+                x = x_next

@@ -68,6 +68,11 @@ def tile_textencoder_b_kernel(tc, emb, gain, shift, w_x, w_gate, w_ff, offs, out
         eps_sb = held.tile([P, 1], F32, name="eps_sb")
         nc.vector.memset(eps_sb[:], EPS)
 
+        scratch = held.tile([P, 1], F32, name="scratch")
+
+        def load_table_after(func, column):
+            nc.scalar.activation(scratch[:], column, func, bias=eps_sb[:, 0:1], scale=0.0)
+
         def look_up(t):
             x = looked_up.tile([P, KB, W], F32, name="x")
             piece = offsets[:, t * (W // 16) : (t + 1) * (W // 16)]
@@ -104,6 +109,7 @@ def tile_textencoder_b_kernel(tc, emb, gain, shift, w_x, w_gate, w_ff, offs, out
             var_ps = average(squares, "var_ps")
             rstd = norm.tile([P, W], F32, name="rstd")
             nc.scalar.activation(rstd[:], var_ps[:], ACT.Abs_reciprocal_sqrt, bias=eps_sb[:, 0:1])
+            load_table_after(ACT.Silu, rstd[:, 0:1])
             h = norm.tile([P, KB, W], BF16, name="h")
             for kb in range(KB):
                 unit = block.tile([P, W], F32, name="unit")
@@ -126,6 +132,7 @@ def tile_textencoder_b_kernel(tc, emb, gain, shift, w_x, w_gate, w_ff, offs, out
                 silu = stage.tile([P, W], F32, name="silu")
                 nc.scalar.activation(silu[:], z_ps[:], ACT.Silu)
                 nc.vector.tensor_tensor(gated[:, fb, :], silu[:], u_ps[:], ALU.mult)
+            return silu
 
         def down(t, x, gated):
             for cb in range(KB):
@@ -139,6 +146,7 @@ def tile_textencoder_b_kernel(tc, emb, gain, shift, w_x, w_gate, w_ff, offs, out
                 nc.vector.tensor_tensor(result[:], o_ps[:], x[:, cb, :], ALU.add)
                 nc.sync.dma_start(out[cb * P : (cb + 1) * P, t * W : (t + 1) * W], result[:])
 
+        load_table_after(ACT.Abs_reciprocal_sqrt, eps_sb[:, 0:1])
         x = look_up(0)
         h = normalise(*centre_and_square(x, tensor_engine_adds=True))
         for t in range(CHUNKS):
@@ -148,8 +156,9 @@ def tile_textencoder_b_kernel(tc, emb, gain, shift, w_x, w_gate, w_ff, offs, out
             if not last:
                 x_next = look_up(t + 1)
                 half_done = centre_and_square(x_next, tensor_engine_adds=False)
-            up(h, gated, range(FB // 2, FB))
+            last_silu = up(h, gated, range(FB // 2, FB))
             if not last:
+                load_table_after(ACT.Abs_reciprocal_sqrt, last_silu[:, 0:1])
                 h = normalise(*half_done)
             down(t, x, gated)
             if not last:

@@ -7,8 +7,9 @@ EPS = 1e-5
 P = 128
 KB = C // P
 FB = F // P
-W = 256
-CHUNKS = N // W
+CHUNK_WIDTHS = (256, 256, 512)
+PIECE = 256
+assert sum(CHUNK_WIDTHS) == N and all(width % PIECE == 0 for width in CHUNK_WIDTHS)
 GROUP = 4
 FLOPS = 2 * C * F * N * 3
 
@@ -73,93 +74,96 @@ def tile_textencoder_b_kernel(tc, emb, gain, shift, w_x, w_gate, w_ff, offs, out
         def load_table_after(func, column):
             nc.scalar.activation(scratch[:], column, func, bias=eps_sb[:, 0:1], scale=0.0)
 
-        def look_up(t):
-            x = looked_up.tile([P, KB, W], F32, name="x")
-            piece = offsets[:, t * (W // 16) : (t + 1) * (W // 16)]
-            for kb in range(KB):
-                nc.scalar.activation(x[:, kb, :], table[kb][:].indirect(piece), ACT.Copy)
+        def look_up(start, width):
+            x = looked_up.tile([P, KB, width], F32, name="x")
+            for first in range(0, width, PIECE):
+                piece = offsets[:, (start + first) // 16 : (start + first + PIECE) // 16]
+                for kb in range(KB):
+                    nc.scalar.activation(x[:, kb, first : first + PIECE], table[kb][:].indirect(piece), ACT.Copy)
             return x
 
-        def add_up(parts):
-            total = norm.tile([P, W], F32, name="total")
+        def add_up(parts, width):
+            total = norm.tile([P, width], F32, name="total")
             nc.vector.tensor_tensor(total[:], parts[0], parts[1], ALU.add)
             for part in parts[2:]:
                 nc.vector.tensor_tensor(total[:], total[:], part, ALU.add)
             return [total[:]]
 
-        def average(parts, name):
-            mean_ps = stat_psum.tile([P, W], F32, name=name)
+        def average(parts, width, name):
+            mean_ps = stat_psum.tile([P, width], F32, name=name)
             for i, part in enumerate(parts):
                 nc.tensor.matmul(mean_ps[:], averager[:], part, start=(i == 0), stop=(i == len(parts) - 1))
             return mean_ps
 
-        def centre_and_square(x, tensor_engine_adds):
+        def centre_and_square(x, width, tensor_engine_adds):
             blocks = [x[:, kb, :] for kb in range(KB)]
-            mean_ps = average(blocks if tensor_engine_adds else add_up(blocks), "mean_ps")
-            centred = norm.tile([P, KB, W], F32, name="centred")
+            mean_ps = average(blocks if tensor_engine_adds else add_up(blocks, width), width, "mean_ps")
+            centred = norm.tile([P, KB, width], F32, name="centred")
             squares = []
             for kb in range(KB):
                 nc.vector.tensor_tensor(centred[:, kb, :], blocks[kb], mean_ps[:], ALU.subtract)
-                square = block.tile([P, W], F32, name="square")
+                square = block.tile([P, width], F32, name="square")
                 nc.scalar.activation(square[:], centred[:, kb, :], ACT.Square)
                 squares.append(square[:])
-            return centred, (squares if tensor_engine_adds else add_up(squares))
+            return centred, (squares if tensor_engine_adds else add_up(squares, width))
 
-        def normalise(centred, squares):
-            var_ps = average(squares, "var_ps")
-            rstd = norm.tile([P, W], F32, name="rstd")
+        def normalise(centred, squares, width):
+            var_ps = average(squares, width, "var_ps")
+            rstd = norm.tile([P, width], F32, name="rstd")
             nc.scalar.activation(rstd[:], var_ps[:], ACT.Abs_reciprocal_sqrt, bias=eps_sb[:, 0:1])
             load_table_after(ACT.Silu, rstd[:, 0:1])
-            h = norm.tile([P, KB, W], BF16, name="h")
+            h = norm.tile([P, KB, width], BF16, name="h")
             for kb in range(KB):
-                unit = block.tile([P, W], F32, name="unit")
+                unit = block.tile([P, width], F32, name="unit")
                 nc.vector.tensor_tensor(unit[:], centred[:, kb, :], rstd[:], ALU.mult)
                 nc.scalar.activation(
                     h[:, kb, :], unit[:], ACT.Identity, bias=shift_sb[:, kb : kb + 1], scale=gain_sb[:, kb : kb + 1]
                 )
             return h
 
-        def up(h, gated, hidden_blocks):
+        def up(h, gated, width, hidden_blocks):
             for fb in hidden_blocks:
                 g, i = divmod(fb, GROUP)
                 f_cols = slice(i * P, (i + 1) * P)
-                z_ps = up_psum.tile([P, W], F32, name="z_ps")
+                z_ps = up_psum.tile([P, width], F32, name="z_ps")
                 for kb in range(KB):
                     nc.tensor.matmul(z_ps[:], wg[g][:, kb, f_cols], h[:, kb, :], start=(kb == 0), stop=(kb == KB - 1))
-                u_ps = up_psum.tile([P, W], F32, name="u_ps")
+                u_ps = up_psum.tile([P, width], F32, name="u_ps")
                 for kb in range(KB):
                     nc.tensor.matmul(u_ps[:], wx[g][:, kb, f_cols], h[:, kb, :], start=(kb == 0), stop=(kb == KB - 1))
-                silu = stage.tile([P, W], F32, name="silu")
+                silu = stage.tile([P, width], F32, name="silu")
                 nc.scalar.activation(silu[:], z_ps[:], ACT.Silu)
                 nc.vector.tensor_tensor(gated[:, fb, :], silu[:], u_ps[:], ALU.mult)
             return silu
 
-        def down(t, x, gated):
+        def down(start, width, x, gated):
             for cb in range(KB):
-                o_ps = down_psum.tile([P, W], F32, name="o_ps")
+                o_ps = down_psum.tile([P, width], F32, name="o_ps")
                 for fb in range(FB):
                     g, i = divmod(fb, GROUP)
                     nc.tensor.matmul(
                         o_ps[:], wf[g][:, i, cb * P : (cb + 1) * P], gated[:, fb, :], start=(fb == 0), stop=(fb == FB - 1)
                     )
-                result = stage.tile([P, W], F32, name="result")
+                result = stage.tile([P, width], F32, name="result")
                 nc.vector.tensor_tensor(result[:], o_ps[:], x[:, cb, :], ALU.add)
-                nc.sync.dma_start(out[cb * P : (cb + 1) * P, t * W : (t + 1) * W], result[:])
+                nc.sync.dma_start(out[cb * P : (cb + 1) * P, start : start + width], result[:])
 
         load_table_after(ACT.Abs_reciprocal_sqrt, eps_sb[:, 0:1])
-        x = look_up(0)
-        h = normalise(*centre_and_square(x, tensor_engine_adds=True))
-        for t in range(CHUNKS):
-            last = t == CHUNKS - 1
-            gated = mlp.tile([P, FB, W], BF16, name="gated")
-            up(h, gated, range(0, FB // 2))
+        chunks = [(sum(CHUNK_WIDTHS[:t]), width) for t, width in enumerate(CHUNK_WIDTHS)]
+        x = look_up(*chunks[0])
+        h = normalise(*centre_and_square(x, chunks[0][1], tensor_engine_adds=True), chunks[0][1])
+        for t, (start, width) in enumerate(chunks):
+            last = t == len(chunks) - 1
+            gated = mlp.tile([P, FB, width], BF16, name="gated")
+            up(h, gated, width, range(0, FB // 2))
             if not last:
-                x_next = look_up(t + 1)
-                half_done = centre_and_square(x_next, tensor_engine_adds=False)
-            last_silu = up(h, gated, range(FB // 2, FB))
+                next_width = chunks[t + 1][1]
+                x_next = look_up(*chunks[t + 1])
+                half_done = centre_and_square(x_next, next_width, tensor_engine_adds=False)
+            last_silu = up(h, gated, width, range(FB // 2, FB))
             if not last:
                 load_table_after(ACT.Abs_reciprocal_sqrt, last_silu[:, 0:1])
-                h = normalise(*half_done)
-            down(t, x, gated)
+                h = normalise(*half_done, next_width)
+            down(start, width, x, gated)
             if not last:
                 x = x_next

@@ -1,15 +1,15 @@
 from contextlib import ExitStack
 
 import concourse.mybir as mybir
+from concourse.masks import make_identity
 
 C, S, N, F = 512, 2048, 1024, 2048
 EPS = 1e-5
 P = 128
 KB = C // P
 FB = F // P
-CHUNK_WIDTHS = (256, 256, 512)
-PIECE = 256
-assert sum(CHUNK_WIDTHS) == N and all(width % PIECE == 0 for width in CHUNK_WIDTHS)
+W = 256
+CHUNKS = N // W
 GROUP = 4
 FLOPS = 2 * C * F * N * 3
 
@@ -41,11 +41,15 @@ def tile_textencoder_b_kernel(tc, emb, gain, shift, w_x, w_gate, w_ff, offs, out
             nc.sync.dma_start(table_kb[:], emb[kb * P : (kb + 1) * P, :])
             table.append(table_kb)
 
-        gain_sb = held.tile([P, KB], F32, name="gain_sb")
-        shift_sb = held.tile([P, KB], F32, name="shift_sb")
-        with nc.allow_non_contiguous_dma(reason="512 single floats, one to a partition and block"):
-            nc.scalar.dma_start(gain_sb[:], gain.rearrange("(k p) o -> p (k o)", p=P))
-            nc.scalar.dma_start(shift_sb[:], shift.rearrange("(k p) o -> p (k o)", p=P))
+        rows = held.tile([2 * KB, P], F32, name="rows")
+        nc.scalar.dma_start(rows[0:KB, :], gain.rearrange("(k p) o -> k (p o)", p=P))
+        nc.scalar.dma_start(rows[KB : 2 * KB, :], shift.rearrange("(k p) o -> k (p o)", p=P))
+        identity = held.tile([2 * KB, 2 * KB], F32, name="identity")
+        make_identity(nc, identity[:])
+        columns_ps = stat_psum.tile([P, 2 * KB], F32, name="columns_ps", tag="var_ps")
+        nc.tensor.matmul(columns_ps[:], rows[:], identity[:], start=True, stop=True)
+        gain_shift = held.tile([P, 2 * KB], F32, name="gain_shift")
+        nc.vector.tensor_copy(gain_shift[:], columns_ps[:])
 
         w_gate_view = w_gate.rearrange("(k p) f -> p k f", p=P)
         w_x_view = w_x.rearrange("(k p) f -> p k f", p=P)
@@ -74,96 +78,92 @@ def tile_textencoder_b_kernel(tc, emb, gain, shift, w_x, w_gate, w_ff, offs, out
         def load_table_after(func, column):
             nc.scalar.activation(scratch[:], column, func, bias=eps_sb[:, 0:1], scale=0.0)
 
-        def look_up(start, width):
-            x = looked_up.tile([P, KB, width], F32, name="x")
-            for first in range(0, width, PIECE):
-                piece = offsets[:, (start + first) // 16 : (start + first + PIECE) // 16]
-                for kb in range(KB):
-                    nc.scalar.activation(x[:, kb, first : first + PIECE], table[kb][:].indirect(piece), ACT.Copy)
+        def look_up(t):
+            x = looked_up.tile([P, KB, W], F32, name="x")
+            piece = offsets[:, t * (W // 16) : (t + 1) * (W // 16)]
+            for kb in range(KB):
+                nc.scalar.activation(x[:, kb, :], table[kb][:].indirect(piece), ACT.Copy)
             return x
 
-        def add_up(parts, width):
-            total = norm.tile([P, width], F32, name="total")
+        def add_up(parts):
+            total = norm.tile([P, W], F32, name="total")
             nc.vector.tensor_tensor(total[:], parts[0], parts[1], ALU.add)
             for part in parts[2:]:
                 nc.vector.tensor_tensor(total[:], total[:], part, ALU.add)
             return [total[:]]
 
-        def average(parts, width, name):
-            mean_ps = stat_psum.tile([P, width], F32, name=name)
+        def average(parts, name):
+            mean_ps = stat_psum.tile([P, W], F32, name=name)
             for i, part in enumerate(parts):
                 nc.tensor.matmul(mean_ps[:], averager[:], part, start=(i == 0), stop=(i == len(parts) - 1))
             return mean_ps
 
-        def centre_and_square(x, width, tensor_engine_adds):
+        def centre_and_square(x, tensor_engine_adds):
             blocks = [x[:, kb, :] for kb in range(KB)]
-            mean_ps = average(blocks if tensor_engine_adds else add_up(blocks, width), width, "mean_ps")
-            centred = norm.tile([P, KB, width], F32, name="centred")
+            mean_ps = average(blocks if tensor_engine_adds else add_up(blocks), "mean_ps")
+            centred = norm.tile([P, KB, W], F32, name="centred")
             squares = []
             for kb in range(KB):
                 nc.vector.tensor_tensor(centred[:, kb, :], blocks[kb], mean_ps[:], ALU.subtract)
-                square = block.tile([P, width], F32, name="square")
+                square = block.tile([P, W], F32, name="square")
                 nc.scalar.activation(square[:], centred[:, kb, :], ACT.Square)
                 squares.append(square[:])
-            return centred, (squares if tensor_engine_adds else add_up(squares, width))
+            return centred, (squares if tensor_engine_adds else add_up(squares))
 
-        def normalise(centred, squares, width):
-            var_ps = average(squares, width, "var_ps")
-            rstd = norm.tile([P, width], F32, name="rstd")
+        def normalise(centred, squares):
+            var_ps = average(squares, "var_ps")
+            rstd = norm.tile([P, W], F32, name="rstd")
             nc.scalar.activation(rstd[:], var_ps[:], ACT.Abs_reciprocal_sqrt, bias=eps_sb[:, 0:1])
             load_table_after(ACT.Silu, rstd[:, 0:1])
-            h = norm.tile([P, KB, width], BF16, name="h")
+            h = norm.tile([P, KB, W], BF16, name="h")
             for kb in range(KB):
-                unit = block.tile([P, width], F32, name="unit")
+                unit = block.tile([P, W], F32, name="unit")
                 nc.vector.tensor_tensor(unit[:], centred[:, kb, :], rstd[:], ALU.mult)
-                nc.scalar.activation(
-                    h[:, kb, :], unit[:], ACT.Identity, bias=shift_sb[:, kb : kb + 1], scale=gain_sb[:, kb : kb + 1]
-                )
+                gain_kb, shift_kb = gain_shift[:, kb : kb + 1], gain_shift[:, KB + kb : KB + kb + 1]
+                nc.scalar.activation(h[:, kb, :], unit[:], ACT.Identity, bias=shift_kb, scale=gain_kb)
             return h
 
-        def up(h, gated, width, hidden_blocks):
+        def up(h, gated, hidden_blocks):
             for fb in hidden_blocks:
                 g, i = divmod(fb, GROUP)
                 f_cols = slice(i * P, (i + 1) * P)
-                z_ps = up_psum.tile([P, width], F32, name="z_ps")
+                z_ps = up_psum.tile([P, W], F32, name="z_ps")
                 for kb in range(KB):
                     nc.tensor.matmul(z_ps[:], wg[g][:, kb, f_cols], h[:, kb, :], start=(kb == 0), stop=(kb == KB - 1))
-                u_ps = up_psum.tile([P, width], F32, name="u_ps")
+                u_ps = up_psum.tile([P, W], F32, name="u_ps")
                 for kb in range(KB):
                     nc.tensor.matmul(u_ps[:], wx[g][:, kb, f_cols], h[:, kb, :], start=(kb == 0), stop=(kb == KB - 1))
-                silu = stage.tile([P, width], F32, name="silu")
+                silu = stage.tile([P, W], F32, name="silu")
                 nc.scalar.activation(silu[:], z_ps[:], ACT.Silu)
                 nc.vector.tensor_tensor(gated[:, fb, :], silu[:], u_ps[:], ALU.mult)
             return silu
 
-        def down(start, width, x, gated):
+        def down(t, x, gated):
             for cb in range(KB):
-                o_ps = down_psum.tile([P, width], F32, name="o_ps")
+                o_ps = down_psum.tile([P, W], F32, name="o_ps")
                 for fb in range(FB):
                     g, i = divmod(fb, GROUP)
                     nc.tensor.matmul(
                         o_ps[:], wf[g][:, i, cb * P : (cb + 1) * P], gated[:, fb, :], start=(fb == 0), stop=(fb == FB - 1)
                     )
-                result = stage.tile([P, width], F32, name="result")
+                result = stage.tile([P, W], F32, name="result")
                 nc.vector.tensor_tensor(result[:], o_ps[:], x[:, cb, :], ALU.add)
-                nc.sync.dma_start(out[cb * P : (cb + 1) * P, start : start + width], result[:])
+                nc.sync.dma_start(out[cb * P : (cb + 1) * P, t * W : (t + 1) * W], result[:])
 
         load_table_after(ACT.Abs_reciprocal_sqrt, eps_sb[:, 0:1])
-        chunks = [(sum(CHUNK_WIDTHS[:t]), width) for t, width in enumerate(CHUNK_WIDTHS)]
-        x = look_up(*chunks[0])
-        h = normalise(*centre_and_square(x, chunks[0][1], tensor_engine_adds=True), chunks[0][1])
-        for t, (start, width) in enumerate(chunks):
-            last = t == len(chunks) - 1
-            gated = mlp.tile([P, FB, width], BF16, name="gated")
-            up(h, gated, width, range(0, FB // 2))
+        x = look_up(0)
+        h = normalise(*centre_and_square(x, tensor_engine_adds=True))
+        for t in range(CHUNKS):
+            last = t == CHUNKS - 1
+            gated = mlp.tile([P, FB, W], BF16, name="gated")
+            up(h, gated, range(0, FB // 2))
             if not last:
-                next_width = chunks[t + 1][1]
-                x_next = look_up(*chunks[t + 1])
-                half_done = centre_and_square(x_next, next_width, tensor_engine_adds=False)
-            last_silu = up(h, gated, width, range(FB // 2, FB))
+                x_next = look_up(t + 1)
+                half_done = centre_and_square(x_next, tensor_engine_adds=False)
+            last_silu = up(h, gated, range(FB // 2, FB))
             if not last:
                 load_table_after(ACT.Abs_reciprocal_sqrt, last_silu[:, 0:1])
-                h = normalise(*half_done, next_width)
-            down(start, width, x, gated)
+                h = normalise(*half_done)
+            down(t, x, gated)
             if not last:
                 x = x_next

@@ -29,8 +29,7 @@ def tile_textencoder_b_kernel(tc, emb, gain, shift, w_x, w_gate, w_ff, offs, out
         block = ctx.enter_context(tc.tile_pool(name="block", bufs=4))
         mlp = ctx.enter_context(tc.tile_pool(name="mlp", bufs=2))
         stage = ctx.enter_context(tc.tile_pool(name="stage", bufs=3))
-        stat_psum = ctx.enter_context(tc.psum_pool(name="stat_psum", bufs=1))
-        up_psum = ctx.enter_context(tc.psum_pool(name="up_psum", bufs=2))
+        ring_psum = ctx.enter_context(tc.psum_pool(name="ring_psum", bufs=6))
         down_psum = ctx.enter_context(tc.psum_pool(name="down_psum", bufs=2))
 
         offsets = held.tile([P, N // 16], U16, name="offsets")
@@ -46,7 +45,7 @@ def tile_textencoder_b_kernel(tc, emb, gain, shift, w_x, w_gate, w_ff, offs, out
         nc.scalar.dma_start(rows[KB : 2 * KB, :], shift.rearrange("(k p) o -> k (p o)", p=P))
         identity = held.tile([2 * KB, 2 * KB], F32, name="identity")
         make_identity(nc, identity[:])
-        columns_ps = stat_psum.tile([P, 2 * KB], F32, name="columns_ps", tag="var_ps")
+        columns_ps = ring_psum.tile([P, 2 * KB], F32, name="columns_ps", tag="ring")
         nc.tensor.matmul(columns_ps[:], rows[:], identity[:], start=True, stop=True)
         gain_shift = held.tile([P, 2 * KB], F32, name="gain_shift")
         nc.vector.tensor_copy(gain_shift[:], columns_ps[:])
@@ -78,11 +77,14 @@ def tile_textencoder_b_kernel(tc, emb, gain, shift, w_x, w_gate, w_ff, offs, out
         def load_table_after(func, column):
             nc.scalar.activation(scratch[:], column, func, bias=eps_sb[:, 0:1], scale=0.0)
 
+        def look_up_block(x, t, kb):
+            piece = offsets[:, t * (W // 16) : (t + 1) * (W // 16)]
+            nc.scalar.activation(x[:, kb, :], table[kb][:].indirect(piece), ACT.Copy)
+
         def look_up(t):
             x = looked_up.tile([P, KB, W], F32, name="x")
-            piece = offsets[:, t * (W // 16) : (t + 1) * (W // 16)]
             for kb in range(KB):
-                nc.scalar.activation(x[:, kb, :], table[kb][:].indirect(piece), ACT.Copy)
+                look_up_block(x, t, kb)
             return x
 
         def add_up(parts):
@@ -93,14 +95,13 @@ def tile_textencoder_b_kernel(tc, emb, gain, shift, w_x, w_gate, w_ff, offs, out
             return [total[:]]
 
         def average(parts, name):
-            mean_ps = stat_psum.tile([P, W], F32, name=name)
+            mean_ps = ring_psum.tile([P, W], F32, name=name, tag="ring")
             for i, part in enumerate(parts):
                 nc.tensor.matmul(mean_ps[:], averager[:], part, start=(i == 0), stop=(i == len(parts) - 1))
             return mean_ps
 
-        def centre_and_square(x, tensor_engine_adds):
+        def centre_and_square(x, mean_ps, tensor_engine_adds):
             blocks = [x[:, kb, :] for kb in range(KB)]
-            mean_ps = average(blocks if tensor_engine_adds else add_up(blocks), "mean_ps")
             centred = norm.tile([P, KB, W], F32, name="centred")
             squares = []
             for kb in range(KB):
@@ -114,23 +115,23 @@ def tile_textencoder_b_kernel(tc, emb, gain, shift, w_x, w_gate, w_ff, offs, out
             var_ps = average(squares, "var_ps")
             rstd = norm.tile([P, W], F32, name="rstd")
             nc.scalar.activation(rstd[:], var_ps[:], ACT.Abs_reciprocal_sqrt, bias=eps_sb[:, 0:1])
-            load_table_after(ACT.Silu, rstd[:, 0:1])
             h = norm.tile([P, KB, W], BF16, name="h")
             for kb in range(KB):
                 unit = block.tile([P, W], F32, name="unit")
                 nc.vector.tensor_tensor(unit[:], centred[:, kb, :], rstd[:], ALU.mult)
                 gain_kb, shift_kb = gain_shift[:, kb : kb + 1], gain_shift[:, KB + kb : KB + kb + 1]
                 nc.scalar.activation(h[:, kb, :], unit[:], ACT.Identity, bias=shift_kb, scale=gain_kb)
+            load_table_after(ACT.Silu, h[:, KB - 1, 0:1])
             return h
 
         def up(h, gated, hidden_blocks):
             for fb in hidden_blocks:
                 g, i = divmod(fb, GROUP)
                 f_cols = slice(i * P, (i + 1) * P)
-                z_ps = up_psum.tile([P, W], F32, name="z_ps")
+                z_ps = ring_psum.tile([P, W], F32, name="z_ps", tag="ring")
                 for kb in range(KB):
                     nc.tensor.matmul(z_ps[:], wg[g][:, kb, f_cols], h[:, kb, :], start=(kb == 0), stop=(kb == KB - 1))
-                u_ps = up_psum.tile([P, W], F32, name="u_ps")
+                u_ps = ring_psum.tile([P, W], F32, name="u_ps", tag="ring")
                 for kb in range(KB):
                     nc.tensor.matmul(u_ps[:], wx[g][:, kb, f_cols], h[:, kb, :], start=(kb == 0), stop=(kb == KB - 1))
                 silu = stage.tile([P, W], F32, name="silu")
@@ -151,15 +152,25 @@ def tile_textencoder_b_kernel(tc, emb, gain, shift, w_x, w_gate, w_ff, offs, out
                 nc.sync.dma_start(out[cb * P : (cb + 1) * P, t * W : (t + 1) * W], result[:])
 
         load_table_after(ACT.Abs_reciprocal_sqrt, eps_sb[:, 0:1])
-        x = look_up(0)
-        h = normalise(*centre_and_square(x, tensor_engine_adds=True))
+
+        x = looked_up.tile([P, KB, W], F32, name="x")
+        x_next = looked_up.tile([P, KB, W], F32, name="x")
+        mean_ps = ring_psum.tile([P, W], F32, name="mean_ps", tag="ring")
+        mean_next_ps = down_psum.tile([P, W], F32, name="mean_next_ps", tag="o_ps")
+        for kb in range(KB):
+            for t, x_t, mean_t in ((0, x, mean_ps), (1, x_next, mean_next_ps)):
+                look_up_block(x_t, t, kb)
+                nc.tensor.matmul(mean_t[:], averager[:], x_t[:, kb, :], start=(kb == 0), stop=(kb == KB - 1))
+        h = normalise(*centre_and_square(x, mean_ps, tensor_engine_adds=True))
         for t in range(CHUNKS):
             last = t == CHUNKS - 1
             gated = mlp.tile([P, FB, W], BF16, name="gated")
             up(h, gated, range(0, FB // 2))
             if not last:
-                x_next = look_up(t + 1)
-                half_done = centre_and_square(x_next, tensor_engine_adds=False)
+                if t > 0:
+                    x_next = look_up(t + 1)
+                    mean_next_ps = average(add_up([x_next[:, kb, :] for kb in range(KB)]), "mean_ps")
+                half_done = centre_and_square(x_next, mean_next_ps, tensor_engine_adds=False)
             last_silu = up(h, gated, range(FB // 2, FB))
             if not last:
                 load_table_after(ACT.Abs_reciprocal_sqrt, last_silu[:, 0:1])

@@ -8,8 +8,10 @@ EPS = 1e-5
 P = 128
 KB = C // P
 FB = F // P
-W = 256
-CHUNKS = N // W
+WIDTHS = (128, 384, 512)
+STARTS = tuple(sum(WIDTHS[:t]) for t in range(len(WIDTHS)))
+CHUNKS = len(WIDTHS)
+assert sum(WIDTHS) == N
 GROUP = 4
 FLOPS = 2 * C * F * N * 3
 
@@ -78,103 +80,103 @@ def tile_textencoder_b_kernel(tc, emb, gain, shift, w_x, w_gate, w_ff, offs, out
             nc.scalar.activation(scratch[:], column, func, bias=eps_sb[:, 0:1], scale=0.0)
 
         def look_up_block(x, t, kb):
-            piece = offsets[:, t * (W // 16) : (t + 1) * (W // 16)]
+            piece = offsets[:, STARTS[t] // 16 : (STARTS[t] + WIDTHS[t]) // 16]
             nc.scalar.activation(x[:, kb, :], table[kb][:].indirect(piece), ACT.Copy)
 
         def look_up(t):
-            x = looked_up.tile([P, KB, W], F32, name="x")
+            x = looked_up.tile([P, KB, WIDTHS[t]], F32, name="x")
             for kb in range(KB):
                 look_up_block(x, t, kb)
             return x
 
-        def add_up(parts):
-            total = norm.tile([P, W], F32, name="total")
+        def add_up(parts, width):
+            total = norm.tile([P, width], F32, name="total")
             nc.vector.tensor_tensor(total[:], parts[0], parts[1], ALU.add)
             for part in parts[2:]:
                 nc.vector.tensor_tensor(total[:], total[:], part, ALU.add)
             return [total[:]]
 
-        def average(parts, name):
-            mean_ps = ring_psum.tile([P, W], F32, name=name, tag="ring")
+        def average(parts, width, name):
+            mean_ps = ring_psum.tile([P, width], F32, name=name, tag="ring")
             for i, part in enumerate(parts):
                 nc.tensor.matmul(mean_ps[:], averager[:], part, start=(i == 0), stop=(i == len(parts) - 1))
             return mean_ps
 
-        def centre_and_square(x, mean_ps, tensor_engine_adds):
+        def centre_and_square(x, mean_ps, width, tensor_engine_adds):
             blocks = [x[:, kb, :] for kb in range(KB)]
-            centred = norm.tile([P, KB, W], F32, name="centred")
+            centred = norm.tile([P, KB, width], F32, name="centred")
             squares = []
             for kb in range(KB):
                 nc.vector.tensor_tensor(centred[:, kb, :], blocks[kb], mean_ps[:], ALU.subtract)
-                square = block.tile([P, W], F32, name="square")
+                square = block.tile([P, width], F32, name="square")
                 nc.scalar.activation(square[:], centred[:, kb, :], ACT.Square)
                 squares.append(square[:])
-            return centred, (squares if tensor_engine_adds else add_up(squares))
+            return centred, (squares if tensor_engine_adds else add_up(squares, width))
 
-        def normalise(centred, squares):
-            var_ps = average(squares, "var_ps")
-            rstd = norm.tile([P, W], F32, name="rstd")
+        def normalise(centred, squares, width):
+            var_ps = average(squares, width, "var_ps")
+            rstd = norm.tile([P, width], F32, name="rstd")
             nc.scalar.activation(rstd[:], var_ps[:], ACT.Abs_reciprocal_sqrt, bias=eps_sb[:, 0:1])
-            h = norm.tile([P, KB, W], BF16, name="h")
+            h = norm.tile([P, KB, width], BF16, name="h")
             for kb in range(KB):
-                unit = block.tile([P, W], F32, name="unit")
+                unit = block.tile([P, width], F32, name="unit")
                 nc.vector.tensor_tensor(unit[:], centred[:, kb, :], rstd[:], ALU.mult)
                 gain_kb, shift_kb = gain_shift[:, kb : kb + 1], gain_shift[:, KB + kb : KB + kb + 1]
                 nc.scalar.activation(h[:, kb, :], unit[:], ACT.Identity, bias=shift_kb, scale=gain_kb)
             load_table_after(ACT.Silu, h[:, KB - 1, 0:1])
             return h
 
-        def up(h, gated, hidden_blocks):
+        def up(h, gated, width, hidden_blocks):
             for fb in hidden_blocks:
                 g, i = divmod(fb, GROUP)
                 f_cols = slice(i * P, (i + 1) * P)
-                z_ps = ring_psum.tile([P, W], F32, name="z_ps", tag="ring")
+                z_ps = ring_psum.tile([P, width], F32, name="z_ps", tag="ring")
                 for kb in range(KB):
                     nc.tensor.matmul(z_ps[:], wg[g][:, kb, f_cols], h[:, kb, :], start=(kb == 0), stop=(kb == KB - 1))
-                u_ps = ring_psum.tile([P, W], F32, name="u_ps", tag="ring")
+                u_ps = ring_psum.tile([P, width], F32, name="u_ps", tag="ring")
                 for kb in range(KB):
                     nc.tensor.matmul(u_ps[:], wx[g][:, kb, f_cols], h[:, kb, :], start=(kb == 0), stop=(kb == KB - 1))
-                silu = stage.tile([P, W], F32, name="silu")
+                silu = stage.tile([P, width], F32, name="silu")
                 nc.scalar.activation(silu[:], z_ps[:], ACT.Silu)
                 nc.vector.tensor_tensor(gated[:, fb, :], silu[:], u_ps[:], ALU.mult)
             return silu
 
         def down(t, x, gated):
             for cb in range(KB):
-                o_ps = down_psum.tile([P, W], F32, name="o_ps")
+                o_ps = down_psum.tile([P, WIDTHS[t]], F32, name="o_ps")
                 for fb in range(FB):
                     g, i = divmod(fb, GROUP)
                     nc.tensor.matmul(
                         o_ps[:], wf[g][:, i, cb * P : (cb + 1) * P], gated[:, fb, :], start=(fb == 0), stop=(fb == FB - 1)
                     )
-                result = stage.tile([P, W], F32, name="result")
+                result = stage.tile([P, WIDTHS[t]], F32, name="result")
                 nc.vector.tensor_tensor(result[:], o_ps[:], x[:, cb, :], ALU.add)
-                nc.sync.dma_start(out[cb * P : (cb + 1) * P, t * W : (t + 1) * W], result[:])
+                nc.sync.dma_start(out[cb * P : (cb + 1) * P, STARTS[t] : STARTS[t] + WIDTHS[t]], result[:])
 
         load_table_after(ACT.Abs_reciprocal_sqrt, eps_sb[:, 0:1])
 
-        x = looked_up.tile([P, KB, W], F32, name="x")
-        x_next = looked_up.tile([P, KB, W], F32, name="x")
-        mean_ps = ring_psum.tile([P, W], F32, name="mean_ps", tag="ring")
-        mean_next_ps = down_psum.tile([P, W], F32, name="mean_next_ps", tag="o_ps")
+        x = looked_up.tile([P, KB, WIDTHS[0]], F32, name="x")
+        x_next = looked_up.tile([P, KB, WIDTHS[1]], F32, name="x")
+        mean_ps = ring_psum.tile([P, WIDTHS[0]], F32, name="mean_ps", tag="ring")
+        mean_next_ps = down_psum.tile([P, WIDTHS[1]], F32, name="mean_next_ps", tag="o_ps")
         for kb in range(KB):
             for t, x_t, mean_t in ((0, x, mean_ps), (1, x_next, mean_next_ps)):
                 look_up_block(x_t, t, kb)
                 nc.tensor.matmul(mean_t[:], averager[:], x_t[:, kb, :], start=(kb == 0), stop=(kb == KB - 1))
-        h = normalise(*centre_and_square(x, mean_ps, tensor_engine_adds=True))
+        h = normalise(*centre_and_square(x, mean_ps, WIDTHS[0], tensor_engine_adds=True), WIDTHS[0])
         for t in range(CHUNKS):
             last = t == CHUNKS - 1
-            gated = mlp.tile([P, FB, W], BF16, name="gated")
-            up(h, gated, range(0, FB // 2))
+            gated = mlp.tile([P, FB, WIDTHS[t]], BF16, name="gated")
+            up(h, gated, WIDTHS[t], range(0, FB // 2))
             if not last:
                 if t > 0:
                     x_next = look_up(t + 1)
-                    mean_next_ps = average(add_up([x_next[:, kb, :] for kb in range(KB)]), "mean_ps")
-                half_done = centre_and_square(x_next, mean_next_ps, tensor_engine_adds=False)
-            last_silu = up(h, gated, range(FB // 2, FB))
+                    mean_next_ps = average(add_up([x_next[:, kb, :] for kb in range(KB)], WIDTHS[t + 1]), WIDTHS[t + 1], "mean_ps")
+                half_done = centre_and_square(x_next, mean_next_ps, WIDTHS[t + 1], tensor_engine_adds=False)
+            last_silu = up(h, gated, WIDTHS[t], range(FB // 2, FB))
             if not last:
                 load_table_after(ACT.Abs_reciprocal_sqrt, last_silu[:, 0:1])
-                h = normalise(*half_done)
+                h = normalise(*half_done, WIDTHS[t + 1])
             down(t, x, gated)
             if not last:
                 x = x_next

@@ -12,6 +12,7 @@ WIDTHS = (128, 384, 512)
 STARTS = tuple(sum(WIDTHS[:t]) for t in range(len(WIDTHS)))
 CHUNKS = len(WIDTHS)
 assert sum(WIDTHS) == N
+LAST_PIECE = 128
 GROUP = 4
 FLOPS = 2 * C * F * N * 3
 
@@ -117,13 +118,13 @@ def tile_textencoder_b_kernel(tc, emb, gain, shift, w_x, w_gate, w_ff, offs, out
             var_ps = average(squares, width, "var_ps")
             rstd = norm.tile([P, width], F32, name="rstd")
             nc.scalar.activation(rstd[:], var_ps[:], ACT.Abs_reciprocal_sqrt, bias=eps_sb[:, 0:1])
+            load_table_after(ACT.Silu, rstd[:, 0:1])
             h = norm.tile([P, KB, width], BF16, name="h")
             for kb in range(KB):
                 unit = block.tile([P, width], F32, name="unit")
                 nc.vector.tensor_tensor(unit[:], centred[:, kb, :], rstd[:], ALU.mult)
                 gain_kb, shift_kb = gain_shift[:, kb : kb + 1], gain_shift[:, KB + kb : KB + kb + 1]
-                nc.scalar.activation(h[:, kb, :], unit[:], ACT.Identity, bias=shift_kb, scale=gain_kb)
-            load_table_after(ACT.Silu, h[:, KB - 1, 0:1])
+                nc.vector.tensor_scalar(h[:, kb, :], unit[:], gain_kb, shift_kb, ALU.mult, ALU.add)
             return h
 
         def up(h, gated, width, hidden_blocks):
@@ -143,15 +144,19 @@ def tile_textencoder_b_kernel(tc, emb, gain, shift, w_x, w_gate, w_ff, offs, out
 
         def down(t, x, gated):
             for cb in range(KB):
-                o_ps = down_psum.tile([P, WIDTHS[t]], F32, name="o_ps")
-                for fb in range(FB):
-                    g, i = divmod(fb, GROUP)
-                    nc.tensor.matmul(
-                        o_ps[:], wf[g][:, i, cb * P : (cb + 1) * P], gated[:, fb, :], start=(fb == 0), stop=(fb == FB - 1)
-                    )
-                result = stage.tile([P, WIDTHS[t]], F32, name="result")
-                nc.vector.tensor_tensor(result[:], o_ps[:], x[:, cb, :], ALU.add)
-                nc.sync.dma_start(out[cb * P : (cb + 1) * P, STARTS[t] : STARTS[t] + WIDTHS[t]], result[:])
+                last_sum = t == CHUNKS - 1 and cb == KB - 1
+                piece = LAST_PIECE if last_sum else WIDTHS[t]
+                for first in range(0, WIDTHS[t], piece):
+                    cols = slice(first, first + piece)
+                    o_ps = down_psum.tile([P, piece], F32, name="o_ps")
+                    for fb in range(FB):
+                        g, i = divmod(fb, GROUP)
+                        nc.tensor.matmul(
+                            o_ps[:], wf[g][:, i, cb * P : (cb + 1) * P], gated[:, fb, cols], start=(fb == 0), stop=(fb == FB - 1)
+                        )
+                    result = stage.tile([P, piece], F32, name="result")
+                    nc.vector.tensor_tensor(result[:], o_ps[:], x[:, cb, cols], ALU.add)
+                    nc.sync.dma_start(out[cb * P : (cb + 1) * P, STARTS[t] + first : STARTS[t] + first + piece], result[:])
 
         load_table_after(ACT.Abs_reciprocal_sqrt, eps_sb[:, 0:1])
 

@@ -13,7 +13,7 @@ STARTS = tuple(sum(WIDTHS[:t]) for t in range(len(WIDTHS)))
 CHUNKS = len(WIDTHS)
 assert sum(WIDTHS) == N
 LAST_PIECE = 128
-GROUP = 4
+GROUP = 8
 FLOPS = 2 * C * F * N * 3
 
 F32 = mybir.dt.float32

@@ -29,6 +29,7 @@ def tile_textencoder_b_kernel(tc, emb, gain, shift, w_x, w_gate, w_ff, offs, out
         held = ctx.enter_context(tc.tile_pool(name="held", bufs=1))
         looked_up = ctx.enter_context(tc.tile_pool(name="looked_up", bufs=2))
         norm = ctx.enter_context(tc.tile_pool(name="norm", bufs=2))
+        centre = ctx.enter_context(tc.tile_pool(name="centre", bufs=1))
         block = ctx.enter_context(tc.tile_pool(name="block", bufs=4))
         mlp = ctx.enter_context(tc.tile_pool(name="mlp", bufs=2))
         stage = ctx.enter_context(tc.tile_pool(name="stage", bufs=3))
@@ -105,7 +106,7 @@ def tile_textencoder_b_kernel(tc, emb, gain, shift, w_x, w_gate, w_ff, offs, out
 
         def centre_and_square(x, mean_ps, width, tensor_engine_adds):
             blocks = [x[:, kb, :] for kb in range(KB)]
-            centred = norm.tile([P, KB, width], F32, name="centred")
+            centred = centre.tile([P, KB, width], F32, name="centred")
             squares = []
             for kb in range(KB):
                 nc.vector.tensor_tensor(centred[:, kb, :], blocks[kb], mean_ps[:], ALU.subtract)

@@ -33,8 +33,7 @@ def tile_textencoder_b_kernel(tc, emb, gain, shift, w_x, w_gate, w_ff, offs, out
         block = ctx.enter_context(tc.tile_pool(name="block", bufs=4))
         mlp = ctx.enter_context(tc.tile_pool(name="mlp", bufs=2))
         stage = ctx.enter_context(tc.tile_pool(name="stage", bufs=3))
-        ring_psum = ctx.enter_context(tc.psum_pool(name="ring_psum", bufs=6))
-        down_psum = ctx.enter_context(tc.psum_pool(name="down_psum", bufs=2))
+        ring_psum = ctx.enter_context(tc.psum_pool(name="ring_psum", bufs=8))
 
         offsets = held.tile([P, N // 16], U16, name="offsets")
         nc.sync.dma_start(offsets[:], offs)
@@ -149,7 +148,7 @@ def tile_textencoder_b_kernel(tc, emb, gain, shift, w_x, w_gate, w_ff, offs, out
                 piece = LAST_PIECE if last_sum else WIDTHS[t]
                 for first in range(0, WIDTHS[t], piece):
                     cols = slice(first, first + piece)
-                    o_ps = down_psum.tile([P, piece], F32, name="o_ps")
+                    o_ps = ring_psum.tile([P, piece], F32, name="o_ps", tag="ring")
                     for fb in range(FB):
                         g, i = divmod(fb, GROUP)
                         nc.tensor.matmul(
@@ -164,7 +163,7 @@ def tile_textencoder_b_kernel(tc, emb, gain, shift, w_x, w_gate, w_ff, offs, out
         x = looked_up.tile([P, KB, WIDTHS[0]], F32, name="x")
         x_next = looked_up.tile([P, KB, WIDTHS[1]], F32, name="x")
         mean_ps = ring_psum.tile([P, WIDTHS[0]], F32, name="mean_ps", tag="ring")
-        mean_next_ps = down_psum.tile([P, WIDTHS[1]], F32, name="mean_next_ps", tag="o_ps")
+        mean_next_ps = ring_psum.tile([P, WIDTHS[1]], F32, name="mean_next_ps", tag="ring")
         for kb in range(KB):
             for t, x_t, mean_t in ((0, x, mean_ps), (1, x_next, mean_next_ps)):
                 look_up_block(x_t, t, kb)

from contextlib import ExitStack

import concourse.mybir as mybir
from concourse.masks import make_identity

C, S, N, F = 512, 2048, 1024, 2048
EPS = 1e-5
P = 128
KB = C // P
FB = F // P
WIDTHS = (128, 384, 512)
STARTS = tuple(sum(WIDTHS[:t]) for t in range(len(WIDTHS)))
CHUNKS = len(WIDTHS)
assert sum(WIDTHS) == N
LAST_PIECE = 128
GROUP = 8
FLOPS = 2 * C * F * N * 3

F32 = mybir.dt.float32
BF16 = mybir.dt.bfloat16
U16 = mybir.dt.uint16
ACT = mybir.ActivationFunctionType
ALU = mybir.AluOpType


def tile_textencoder_b_kernel(tc, emb, gain, shift, w_x, w_gate, w_ff, offs, out):
    nc = tc.nc
    with ExitStack() as ctx:
        held = ctx.enter_context(tc.tile_pool(name="held", bufs=1))
        looked_up = ctx.enter_context(tc.tile_pool(name="looked_up", bufs=2))
        norm = ctx.enter_context(tc.tile_pool(name="norm", bufs=2))
        centre = ctx.enter_context(tc.tile_pool(name="centre", bufs=1))
        block = ctx.enter_context(tc.tile_pool(name="block", bufs=4))
        mlp = ctx.enter_context(tc.tile_pool(name="mlp", bufs=2))
        stage = ctx.enter_context(tc.tile_pool(name="stage", bufs=3))
        ring_psum = ctx.enter_context(tc.psum_pool(name="ring_psum", bufs=8))

        offsets = held.tile([P, N // 16], U16, name="offsets")
        nc.sync.dma_start(offsets[:], offs)
        table = []
        for kb in range(KB):
            table_kb = held.tile([P, S], F32, name=f"table{kb}")
            nc.sync.dma_start(table_kb[:], emb[kb * P : (kb + 1) * P, :])
            table.append(table_kb)

        rows = held.tile([2 * KB, P], F32, name="rows")
        nc.scalar.dma_start(rows[0:KB, :], gain.rearrange("(k p) o -> k (p o)", p=P))
        nc.scalar.dma_start(rows[KB : 2 * KB, :], shift.rearrange("(k p) o -> k (p o)", p=P))
        identity = held.tile([2 * KB, 2 * KB], F32, name="identity")
        make_identity(nc, identity[:])
        columns_ps = ring_psum.tile([P, 2 * KB], F32, name="columns_ps", tag="ring")
        nc.tensor.matmul(columns_ps[:], rows[:], identity[:], start=True, stop=True)
        gain_shift = held.tile([P, 2 * KB], F32, name="gain_shift")
        nc.vector.tensor_copy(gain_shift[:], columns_ps[:])

        w_gate_view = w_gate.rearrange("(k p) f -> p k f", p=P)
        w_x_view = w_x.rearrange("(k p) f -> p k f", p=P)
        w_ff_view = w_ff.rearrange("(b p) c -> p b c", p=P)
        wg, wx, wf = [], [], []
        for g in range(FB // GROUP):
            f_cols = slice(g * GROUP * P, (g + 1) * GROUP * P)
            wg_g = held.tile([P, KB, GROUP * P], BF16, name=f"wg{g}")
            nc.sync.dma_start(wg_g[:], w_gate_view[:, :, f_cols])
            wg.append(wg_g)
            wx_g = held.tile([P, KB, GROUP * P], BF16, name=f"wx{g}")
            nc.sync.dma_start(wx_g[:], w_x_view[:, :, f_cols])
            wx.append(wx_g)
        for g in range(FB // GROUP):
            wf_g = held.tile([P, GROUP, C], BF16, name=f"wf{g}")
            nc.sync.dma_start(wf_g[:], w_ff_view[:, g * GROUP : (g + 1) * GROUP, :])
            wf.append(wf_g)

        averager = held.tile([P, P], F32, name="averager")
        nc.vector.memset(averager[:], 1.0 / C)
        eps_sb = held.tile([P, 1], F32, name="eps_sb")
        nc.vector.memset(eps_sb[:], EPS)

        scratch = held.tile([P, 1], F32, name="scratch")

        def load_table_after(func, column):
            nc.scalar.activation(scratch[:], column, func, bias=eps_sb[:, 0:1], scale=0.0)

        def look_up_block(x, t, kb):
            piece = offsets[:, STARTS[t] // 16 : (STARTS[t] + WIDTHS[t]) // 16]
            nc.scalar.activation(x[:, kb, :], table[kb][:].indirect(piece), ACT.Copy)

        def look_up(t):
            x = looked_up.tile([P, KB, WIDTHS[t]], F32, name="x")
            for kb in range(KB):
                look_up_block(x, t, kb)
            return x

        def add_up(parts, width):
            total = norm.tile([P, width], F32, name="total")
            nc.vector.tensor_tensor(total[:], parts[0], parts[1], ALU.add)
            for part in parts[2:]:
                nc.vector.tensor_tensor(total[:], total[:], part, ALU.add)
            return [total[:]]

        def average(parts, width, name):
            mean_ps = ring_psum.tile([P, width], F32, name=name, tag="ring")
            for i, part in enumerate(parts):
                nc.tensor.matmul(mean_ps[:], averager[:], part, start=(i == 0), stop=(i == len(parts) - 1))
            return mean_ps

        def centre_and_square(x, mean_ps, width, tensor_engine_adds):
            blocks = [x[:, kb, :] for kb in range(KB)]
            centred = centre.tile([P, KB, width], F32, name="centred")
            squares = []
            for kb in range(KB):
                nc.vector.tensor_tensor(centred[:, kb, :], blocks[kb], mean_ps[:], ALU.subtract)
                square = block.tile([P, width], F32, name="square")
                nc.scalar.activation(square[:], centred[:, kb, :], ACT.Square)
                squares.append(square[:])
            return centred, (squares if tensor_engine_adds else add_up(squares, width))

        def normalise(centred, squares, width):
            var_ps = average(squares, width, "var_ps")
            rstd = norm.tile([P, width], F32, name="rstd")
            nc.scalar.activation(rstd[:], var_ps[:], ACT.Abs_reciprocal_sqrt, bias=eps_sb[:, 0:1])
            load_table_after(ACT.Silu, rstd[:, 0:1])
            h = norm.tile([P, KB, width], BF16, name="h")
            for kb in range(KB):
                unit = block.tile([P, width], F32, name="unit")
                nc.vector.tensor_tensor(unit[:], centred[:, kb, :], rstd[:], ALU.mult)
                gain_kb, shift_kb = gain_shift[:, kb : kb + 1], gain_shift[:, KB + kb : KB + kb + 1]
                nc.vector.tensor_scalar(h[:, kb, :], unit[:], gain_kb, shift_kb, ALU.mult, ALU.add)
            return h

        def up(h, gated, width, hidden_blocks):
            for fb in hidden_blocks:
                g, i = divmod(fb, GROUP)
                f_cols = slice(i * P, (i + 1) * P)
                z_ps = ring_psum.tile([P, width], F32, name="z_ps", tag="ring")
                for kb in range(KB):
                    nc.tensor.matmul(z_ps[:], wg[g][:, kb, f_cols], h[:, kb, :], start=(kb == 0), stop=(kb == KB - 1))
                u_ps = ring_psum.tile([P, width], F32, name="u_ps", tag="ring")
                for kb in range(KB):
                    nc.tensor.matmul(u_ps[:], wx[g][:, kb, f_cols], h[:, kb, :], start=(kb == 0), stop=(kb == KB - 1))
                silu = stage.tile([P, width], F32, name="silu")
                nc.scalar.activation(silu[:], z_ps[:], ACT.Silu)
                nc.vector.tensor_tensor(gated[:, fb, :], silu[:], u_ps[:], ALU.mult)
            return silu

        def down(t, x, gated):
            for cb in range(KB):
                last_sum = t == CHUNKS - 1 and cb == KB - 1
                piece = LAST_PIECE if last_sum else WIDTHS[t]
                for first in range(0, WIDTHS[t], piece):
                    cols = slice(first, first + piece)
                    o_ps = ring_psum.tile([P, piece], F32, name="o_ps", tag="ring")
                    for fb in range(FB):
                        g, i = divmod(fb, GROUP)
                        nc.tensor.matmul(
                            o_ps[:], wf[g][:, i, cb * P : (cb + 1) * P], gated[:, fb, cols], start=(fb == 0), stop=(fb == FB - 1)
                        )
                    result = stage.tile([P, piece], F32, name="result")
                    nc.vector.tensor_tensor(result[:], o_ps[:], x[:, cb, cols], ALU.add)
                    nc.sync.dma_start(out[cb * P : (cb + 1) * P, STARTS[t] + first : STARTS[t] + first + piece], result[:])

        load_table_after(ACT.Abs_reciprocal_sqrt, eps_sb[:, 0:1])

        x = looked_up.tile([P, KB, WIDTHS[0]], F32, name="x")
        x_next = looked_up.tile([P, KB, WIDTHS[1]], F32, name="x")
        mean_ps = ring_psum.tile([P, WIDTHS[0]], F32, name="mean_ps", tag="ring")
        mean_next_ps = ring_psum.tile([P, WIDTHS[1]], F32, name="mean_next_ps", tag="ring")
        for kb in range(KB):
            for t, x_t, mean_t in ((0, x, mean_ps), (1, x_next, mean_next_ps)):
                look_up_block(x_t, t, kb)
                nc.tensor.matmul(mean_t[:], averager[:], x_t[:, kb, :], start=(kb == 0), stop=(kb == KB - 1))
        h = normalise(*centre_and_square(x, mean_ps, WIDTHS[0], tensor_engine_adds=True), WIDTHS[0])
        for t in range(CHUNKS):
            last = t == CHUNKS - 1
            gated = mlp.tile([P, FB, WIDTHS[t]], BF16, name="gated")
            up(h, gated, WIDTHS[t], range(0, FB // 2))
            if not last:
                if t > 0:
                    x_next = look_up(t + 1)
                    mean_next_ps = average(add_up([x_next[:, kb, :] for kb in range(KB)], WIDTHS[t + 1]), WIDTHS[t + 1], "mean_ps")
                half_done = centre_and_square(x_next, mean_next_ps, WIDTHS[t + 1], tensor_engine_adds=False)
            last_silu = up(h, gated, WIDTHS[t], range(FB // 2, FB))
            if not last:
                load_table_after(ACT.Abs_reciprocal_sqrt, last_silu[:, 0:1])
                h = normalise(*half_done, WIDTHS[t + 1])
            down(t, x, gated)
            if not last:
                x = x_next
